import numpy as np
import ml_dtypes


def mxq(x, axis, fmt="e4m3"):
    dtype, down = {"e4m3": (ml_dtypes.float8_e4m3fn, 7), "e5m2": (ml_dtypes.float8_e5m2, 14)}[fmt]
    v = np.moveaxis(np.asarray(x, np.float32).astype(ml_dtypes.bfloat16).astype(np.float64), axis, -1)
    blocks = v.reshape(v.shape[:-1] + (-1, 32))
    amax = np.abs(blocks).max(-1, keepdims=True)
    byte = np.maximum(np.where(amax > 0, np.frexp(amax)[1] - 1 + 127, 0) - down, 1)
    scale = np.exp2(byte - 127.0)
    codes = (blocks / scale).astype(np.float32).astype(dtype).astype(np.float64)
    return np.moveaxis((codes * scale).reshape(v.shape), -1, axis)


WIDE = False


def mx_kscale(k):
    if not WIDE:
        return np.ones(k)
    levels = np.array([10, -10, 5, -5, 0])
    a = np.random.permutation(np.resize(levels, k // 512 * 4)).reshape(k // 512, 4)
    idx = np.arange(k)
    return np.exp2(a[idx // 512, idx % 128 // 32])


BF16 = ml_dtypes.bfloat16


def bf(x):
    return np.asarray(x, np.float32).astype(BF16)


def f64(x):
    return np.asarray(x).astype(np.float64)


E2M1 = np.array([0.0, 0.5, 1.0, 1.5, 2.0, 3.0, 4.0, 6.0, -0.0, -0.5, -1.0, -1.5, -2.0, -3.0, -4.0, -6.0])


def pack_weight(w, fmt):
    k, n = w.shape
    w = f64(bf(w)).reshape(k // 32, 32, n)
    amax = np.abs(w).max(1)
    if fmt == "e4m3":
        byte = np.frexp(amax)[1] - 1 + 127 - 7
    else:
        mant, ex = np.frexp(amax / 6.0)
        byte = np.where(mant > 0.5, ex, ex - 1) + 127
    byte = np.clip(np.where(amax > 0, byte, 1), 1, 254)
    scaled = (w * np.exp2(127.0 - byte)[:, None, :]).reshape(k, n).astype(np.float32)
    by_word = np.ascontiguousarray(scaled.reshape(k // 512, 128, 4, n).transpose(0, 1, 3, 2))
    if fmt == "e4m3":
        words = by_word.astype(ml_dtypes.float8_e4m3fn).view(np.uint8)
    else:
        c = by_word.astype(ml_dtypes.float4_e2m1fn).view(np.uint8) & 0xF
        words = c[..., 0::2] | (c[..., 1::2] << 4)
    return np.ascontiguousarray(words), np.ascontiguousarray(byte.astype(np.uint8).reshape(k // 512, 16, n))


def unpack_weight(words, scales, fmt):
    g, p, n, _ = words.shape
    if fmt == "e4m3":
        vals = np.ascontiguousarray(words).view(ml_dtypes.float8_e4m3fn).astype(np.float64)
    else:
        nib = np.empty((g, p, n, 4), np.uint8)
        nib[..., 0::2] = words & 0xF
        nib[..., 1::2] = words >> 4
        vals = E2M1[nib]
    vals = vals * np.repeat(np.exp2(scales.astype(np.float64) - 127.0), 8, axis=1)[..., None]
    return vals.transpose(0, 1, 3, 2).reshape(g * 512, n)


B, GH, GW, E, H, DH = 4, 8, 8, 16384, 8, 64
S = GH * GW
N = H * DH
BASE = 100.0
FMT = "e4m3"


def rope_half(xh, ang):
    x1, x2 = xh[..., 0::2], xh[..., 1::2]
    cos = np.cos(ang)[None, :, None, :]
    sin = np.sin(ang)[None, :, None, :]
    o1 = x1 * cos - x2 * sin
    o2 = x1 * sin + x2 * cos
    return np.stack([o1, o2], axis=-1).reshape(xh.shape)


def rope_2d(t):
    dh = DH // 2
    rows = f64(np.repeat(np.arange(GH), GW))
    cols = f64(np.tile(np.arange(GW), GH))
    inv_freq = BASE ** (-f64(np.arange(0, dh, 2)) / dh)
    ang_r = rows[:, None] * inv_freq[None, :]
    ang_c = cols[:, None] * inv_freq[None, :]
    tr = rope_half(t[..., :dh], ang_r)
    tc = rope_half(t[..., dh:], ang_c)
    return np.concatenate([tr, tc], axis=-1)


def setup_inputs():
    s = mx_kscale(E)
    w = 1.0 / np.sqrt(E)
    x = bf(np.random.standard_normal((B, S, E)) * s)
    Wq_words, Wq_scales = pack_weight(np.random.standard_normal((E, N)) * w / s[:, None], FMT)
    bq = bf(np.random.standard_normal(N) * 0.3)
    Wk_words, Wk_scales = pack_weight(np.random.standard_normal((E, N)) * w / s[:, None], FMT)
    bk = bf(np.random.standard_normal(N) * 0.3)
    return {"x": x,
            "Wq_words": Wq_words,
            "Wq_scales": Wq_scales,
            "bq": bq,
            "Wk_words": Wk_words,
            "Wk_scales": Wk_scales,
            "bk": bk}


def reference(x, Wq_words, Wq_scales, bq, Wk_words, Wk_scales, bk):
    xq = mxq(f64(x), 2, "e4m3")
    q = ((xq @ unpack_weight(Wq_words, Wq_scales, FMT)) + f64(bq)).reshape(B, S, H, DH)
    k = ((xq @ unpack_weight(Wk_words, Wk_scales, FMT)) + f64(bk)).reshape(B, S, H, DH)
    return rope_2d(q), rope_2d(k)

@@ -1,0 +1,244 @@
+import math
+from contextlib import ExitStack
+
+import concourse.mybir as mybir
+from concourse.masks import make_identity
+
+F32 = mybir.dt.float32
+BF16 = mybir.dt.bfloat16
+I32 = mybir.dt.int32
+U32 = mybir.dt.uint32
+U8 = mybir.dt.uint8
+FP8X4 = mybir.dt.float8_e4m3fn_x4
+ALU = mybir.AluOpType
+ACT = mybir.ActivationFunctionType
+
+P = 128
+TOKENS = 256
+TOKEN_TILES = TOKENS // P
+E = 16384
+K_PASS = 512
+GROUPS = E // K_PASS
+N = 512
+HEADS = 8
+HEAD_DIM = 64
+PAIRS = HEAD_DIM // 2
+FREQS = PAIRS // 2
+GRID = 8
+BASE = 100.0
+
+CHUNK = 4
+CHUNKS = GROUPS // CHUNK
+PIECE = 2
+PIECES = GROUPS // PIECE
+PLANES_PER_OFFSET = GROUPS // 4
+
+FLOPS = 2 * TOKENS * E * 2 * N
+
+
+def tile_attention_pa_k_kernel(tc, x, Wq_words, Wq_scales, bq, Wk_words, Wk_scales, bk, out_0, out_1):
+    nc = tc.nc
+    x_rows = x.flatten_outer_dims().rearrange("(m p) k -> p m k", p=P)
+    words = [w.rearrange("g p n t -> p g (n t)") for w in (Wq_words, Wk_words)]
+    scales = [Wq_scales, Wk_scales]
+    biases = [bq, bk]
+    outs = [o.rearrange("b s h d -> (b s) (h d)") for o in (out_0, out_1)]
+
+    with ExitStack() as ctx:
+        ctx.enter_context(tc.manual_schedule())
+        const = ctx.enter_context(tc.tile_pool(name="const", bufs=1))
+        x_pool = ctx.enter_context(tc.tile_pool(name="x_pool", bufs=4))
+        w_pool = ctx.enter_context(tc.tile_pool(name="w_pool", bufs=PIECES))
+        q_pool = ctx.enter_context(tc.tile_pool(name="q_pool", bufs=2))
+        end_pool = ctx.enter_context(tc.tile_pool(name="end_pool", bufs=2))
+        acc_pool = ctx.enter_context(tc.psum_pool(name="acc_pool", bufs=1))
+        t_pool = ctx.enter_context(tc.psum_pool(name="t_pool", bufs=CHUNK))
+
+        x_tiles = {}
+        x_sorted = {}
+        w_tiles = {}
+
+        def load_x(c):
+            x_sb = x_pool.tile([P, TOKEN_TILES, CHUNK * K_PASS], BF16, name="x_sb")
+            nc.sync.dma_start(out=x_sb[:], in_=x_rows[:, :, c * CHUNK * K_PASS : (c + 1) * CHUNK * K_PASS])
+            x_tiles[c] = x_sb
+
+        def load_w(w, piece):
+            w_sb = w_pool.tile([P, PIECE, N], U32, name="w_sb", align_bytes=64)
+            nc.sync.dma_start(
+                out=w_sb[:].bitcast(I32),
+                in_=words[w][:, piece * PIECE : (piece + 1) * PIECE, :].bitcast(I32),
+            )
+            w_tiles[(w, piece)] = w_sb
+
+        def load_w_of_chunk(w, c):
+            for piece in range(c * CHUNK // PIECE, (c + 1) * CHUNK // PIECE):
+                load_w(w, piece)
+
+        load_x(0)
+
+        bias_row = const.tile([P, 2, N], BF16)
+        nc.vector.memset(bias_row[:], 0.0)
+        for w in range(2):
+            nc.scalar.dma_start(out=bias_row[0:1, w, :], in_=biases[w].unsqueeze(0))
+
+        w_planes = []
+        for w in range(2):
+            planes = const.tile([P, PLANES_PER_OFFSET, N], U8, name="planes%d" % w, align_bytes=64)
+            nc.vector.memset(planes[:].rearrange("p c n -> p (c n)").bitcast(I32), 0)
+            w_planes.append(planes)
+
+        def load_scale_rows(w, queue, view):
+            by_offset = scales[w].rearrange("(j c) q n -> j c q n", j=4)
+            for q in range(16):
+                first_row = 32 * (q // 4) + q % 4
+                queue.dma_start(
+                    out=w_planes[w][first_row : first_row + 16 : 4, :, :].bitcast(view),
+                    in_=by_offset[:, :, q, :].bitcast(view),
+                )
+
+        load_scale_rows(0, nc.sync, I32)
+        load_x(1)
+        load_w_of_chunk(0, 0)
+
+        p_index = const.tile([P, 1], I32)
+        nc.gpsimd.iota(p_index[:], pattern=[[0, 1]], base=0, channel_multiplier=1)
+        j_index = const.tile([P, FREQS], I32)
+        nc.gpsimd.iota(j_index[:], pattern=[[1, FREQS]], base=0, channel_multiplier=0)
+        ident = const.tile([P, P], F32)
+        make_identity(nc, ident[:])
+
+        load_scale_rows(1, nc.gpsimd, F32)
+
+        ones = const.tile([P, P], BF16)
+        nc.vector.memset(ones[:], 1.0)
+        bias_all = const.tile([P, 2, N], F32)
+        for w in range(2):
+            bias_ps = t_pool.tile([P, N], F32, name="bias_ps", tag="xt")
+            nc.tensor.matmul(out=bias_ps[:], lhsT=ones[:], rhs=bias_row[:, w, :], start=True, stop=True)
+            nc.vector.tensor_copy(out=bias_all[:, w, :], in_=bias_ps[:])
+
+        pos_int = const.tile([P, 2], I32)
+        nc.vector.tensor_scalar(
+            out=pos_int[:, 0:1], in0=p_index[:], scalar1=3, scalar2=GRID - 1,
+            op0=ALU.logical_shift_right, op1=ALU.bitwise_and,
+        )
+        nc.vector.tensor_single_scalar(out=pos_int[:, 1:2], in_=p_index[:], scalar=GRID - 1, op=ALU.bitwise_and)
+        pos = const.tile([P, 2], F32)
+        nc.vector.tensor_copy(out=pos[:], in_=pos_int[:])
+        j_float = const.tile([P, FREQS], F32)
+        nc.vector.tensor_copy(out=j_float[:], in_=j_index[:])
+        freq = const.tile([P, FREQS], F32)
+        nc.scalar.activation(out=freq[:], in_=j_float[:], func=ACT.Exp, scale=-math.log(BASE) / FREQS)
+        angle = const.tile([P, 2, 2, FREQS], F32)
+        for half in range(2):
+            nc.vector.tensor_scalar(
+                out=angle[:, 1, half, :], in0=freq[:], scalar1=pos[:, half : half + 1], scalar2=None, op0=ALU.mult
+            )
+        nc.vector.tensor_scalar_add(out=angle[:, 0], in0=angle[:, 1], scalar1=math.pi / 2)
+        turn = const.tile([P, 2, 2, FREQS], F32)
+        nc.vector.tensor_scalar(
+            out=turn[:], in0=angle[:], scalar1=math.pi, scalar2=2 * math.pi, op0=ALU.is_gt, op1=ALU.mult
+        )
+        nc.vector.tensor_sub(out=angle[:], in0=angle[:], in1=turn[:])
+        cos_sin = const.tile([P, 2, PAIRS], F32)
+        nc.scalar.activation(out=cos_sin[:], in_=angle[:].rearrange("p f a j -> p f (a j)"), func=ACT.Sin)
+        cos_both = const.tile([P, PAIRS, 2], F32)
+        nc.vector.tensor_copy(out=cos_both[:], in_=cos_sin[:, 0, :].unsqueeze(2).to_broadcast([P, PAIRS, 2]))
+        minus_sin = const.tile([P, PAIRS], F32)
+        nc.vector.tensor_scalar_mul(out=minus_sin[:], in0=cos_sin[:, 1, :], scalar1=-1.0)
+
+        cos_heads = cos_both[:].rearrange("p i e -> p (i e)").unsqueeze(1).to_broadcast([P, HEADS, HEAD_DIM])
+        sin_heads = cos_sin[:, 1, :].unsqueeze(1).to_broadcast([P, HEADS, PAIRS])
+        minus_sin_heads = minus_sin[:].unsqueeze(1).to_broadcast([P, HEADS, PAIRS])
+
+        acc = {}
+        for w in range(2):
+            for m in range(TOKEN_TILES):
+                acc[(w, m)] = acc_pool.tile([P, N], F32, name="acc_%d_%d" % (w, m))
+
+        codes = const.tile([P, GROUPS, TOKEN_TILES, P], U32, align_bytes=64)
+        x_plane = const.tile([P, GROUPS, TOKEN_TILES, P], U8, align_bytes=64)
+
+        def sort_words(c):
+            in_order = q_pool.tile([P, TOKEN_TILES, CHUNK, 2, P], F32, name="in_order")
+            nc.vector.tensor_copy(
+                out=in_order[:],
+                in_=x_tiles[c][:].bitcast(F32).rearrange("r m (g v u) -> r m g u v", g=CHUNK, u=2),
+            )
+            x_sorted[c] = in_order
+
+        def transpose_and_quantise(c):
+            in_order = x_sorted[c]
+            grouped = q_pool.tile([P, CHUNK, TOKEN_TILES, P, 4], BF16, name="grouped", align_bytes=64)
+            for g in range(CHUNK):
+                xt = t_pool.tile([P, TOKEN_TILES, 2, P], F32, name="xt", tag="xt")
+                for m in range(TOKEN_TILES):
+                    for u in range(2):
+                        nc.tensor.transpose(xt[:, m, u, :], in_order[:, m, g, u, :], ident[:])
+                nc.scalar.copy(out=grouped[:, g].bitcast(F32), in_=xt[:].rearrange("p m u r -> p m r u"))
+            groups = slice(c * CHUNK, (c + 1) * CHUNK)
+            nc.vector.quantize_mx(
+                out=codes[:, groups].rearrange("p g m r -> p (g m r)").bitcast(FP8X4),
+                scales=x_plane[:, groups].rearrange("p g m r -> p (g m r)"),
+                in_=grouped[:].rearrange("p g m r t -> p (g m r t)"),
+            )
+
+        def multiply(w, piece):
+            w_sb = w_tiles[(w, piece)]
+            for m in range(TOKEN_TILES):
+                for g in range(PIECE):
+                    group = piece * PIECE + g
+                    offset = 4 * (group // PLANES_PER_OFFSET)
+                    nc.tensor.matmul_mx(
+                        out=acc[(w, m)][:],
+                        lhsT=codes[:, group, m, :].bitcast(FP8X4),
+                        lhsT_scale=x_plane[:, group, m, :],
+                        rhs=w_sb[:, g, :].bitcast(FP8X4),
+                        rhs_scale=w_planes[w][offset:P, group % PLANES_PER_OFFSET, :],
+                        start=(group == 0),
+                        stop=(group == GROUPS - 1),
+                    )
+
+        def finish(w, m):
+            y = end_pool.tile([P, N], F32, name="y")
+            nc.vector.tensor_add(out=y[:], in0=acc[(w, m)][:], in1=bias_all[:, w, :])
+            straight = end_pool.tile([P, N], F32, name="straight")
+            nc.vector.tensor_mul(
+                out=straight[:].rearrange("p (h d) -> p h d", h=HEADS),
+                in0=y[:].rearrange("p (h d) -> p h d", h=HEADS),
+                in1=cos_heads,
+            )
+            y_pairs = y[:].rearrange("p (h i e) -> p e h i", h=HEADS, e=2)
+            crossed = end_pool.tile([P, 2, HEADS, PAIRS], F32, name="crossed")
+            nc.vector.tensor_mul(out=crossed[:, 0], in0=y_pairs[:, 1], in1=minus_sin_heads)
+            nc.vector.tensor_mul(out=crossed[:, 1], in0=y_pairs[:, 0], in1=sin_heads)
+            rotated = end_pool.tile([P, N], F32, name="rotated")
+            nc.vector.tensor_add(
+                out=rotated[:].rearrange("p (n e) -> p n e", e=2),
+                in0=straight[:].rearrange("p (n e) -> p n e", e=2),
+                in1=crossed[:].rearrange("p e h i -> p (h i) e"),
+            )
+            nc.sync.dma_start(out=outs[w][m * P : (m + 1) * P, :], in_=rotated[:])
+
+        sort_words(0)
+        sort_words(1)
+        transpose_and_quantise(0)
+        for c in range(CHUNKS):
+            if c + 2 < CHUNKS:
+                load_x(c + 2)
+                sort_words(c + 2)
+            if c + 1 < CHUNKS:
+                load_w_of_chunk(0, c + 1)
+                transpose_and_quantise(c + 1)
+            for piece in range(c * CHUNK // PIECE, (c + 1) * CHUNK // PIECE):
+                multiply(0, piece)
+
+        for piece in range(PIECES):
+            load_w(1, piece)
+        for m in range(TOKEN_TILES):
+            finish(0, m)
+        for piece in range(PIECES):
+            multiply(1, piece)
+        for m in range(TOKEN_TILES):
+            finish(1, m)

@@ -20,7 +20,10 @@ E = 16384
 K_PASS = 512
 GROUPS = E // K_PASS
 N = 512
+N_PART = N // 2
+PARTS = N // N_PART
 HEADS = 8
+PART_HEADS = HEADS // PARTS
 HEAD_DIM = 64
 PAIRS = HEAD_DIM // 2
 FREQS = PAIRS // 2
@@ -29,8 +32,10 @@ BASE = 100.0
 
 CHUNK = 4
 CHUNKS = GROUPS // CHUNK
+LEAD = 3
 PIECE = 2
 PIECES = GROUPS // PIECE
+LAST_PIECES = 4
 PLANES_PER_OFFSET = GROUPS // 4
 
 FLOPS = 2 * TOKENS * E * 2 * N
@@ -52,10 +57,11 @@ def tile_attention_pa_k_kernel(tc, x, Wq_words, Wq_scales, bq, Wk_words, Wk_scal
         q_pool = ctx.enter_context(tc.tile_pool(name="q_pool", bufs=2))
         end_pool = ctx.enter_context(tc.tile_pool(name="end_pool", bufs=2))
         acc_pool = ctx.enter_context(tc.psum_pool(name="acc_pool", bufs=1))
-        t_pool = ctx.enter_context(tc.psum_pool(name="t_pool", bufs=CHUNK))
+        t_pool = ctx.enter_context(tc.psum_pool(name="t_pool", bufs=6))
 
         x_tiles = {}
         x_sorted = {}
+        x_grouped = {}
         w_tiles = {}
 
         def load_x(c):
@@ -63,24 +69,19 @@ def tile_attention_pa_k_kernel(tc, x, Wq_words, Wq_scales, bq, Wk_words, Wk_scal
             nc.sync.dma_start(out=x_sb[:], in_=x_rows[:, :, c * CHUNK * K_PASS : (c + 1) * CHUNK * K_PASS])
             x_tiles[c] = x_sb
 
-        def load_w(w, piece):
-            w_sb = w_pool.tile([P, PIECE, N], U32, name="w_sb", align_bytes=64)
+        def load_w(w, piece, first_column=0, columns=N):
+            w_sb = w_pool.tile([P, PIECE, columns], U32, name="w_sb", align_bytes=64)
             nc.sync.dma_start(
                 out=w_sb[:].bitcast(I32),
-                in_=words[w][:, piece * PIECE : (piece + 1) * PIECE, :].bitcast(I32),
+                in_=words[w][
+                    :, piece * PIECE : (piece + 1) * PIECE, 4 * first_column : 4 * (first_column + columns)
+                ].bitcast(I32),
             )
-            w_tiles[(w, piece)] = w_sb
+            w_tiles[(w, piece, first_column)] = w_sb
 
         def load_w_of_chunk(w, c):
             for piece in range(c * CHUNK // PIECE, (c + 1) * CHUNK // PIECE):
                 load_w(w, piece)
-
-        load_x(0)
-
-        bias_row = const.tile([P, 2, N], BF16)
-        nc.vector.memset(bias_row[:], 0.0)
-        for w in range(2):
-            nc.scalar.dma_start(out=bias_row[0:1, w, :], in_=biases[w].unsqueeze(0))
 
         w_planes = []
         for w in range(2):
@@ -88,18 +89,26 @@ def tile_attention_pa_k_kernel(tc, x, Wq_words, Wq_scales, bq, Wk_words, Wk_scal
             nc.vector.memset(planes[:].rearrange("p c n -> p (c n)").bitcast(I32), 0)
             w_planes.append(planes)
 
-        def load_scale_rows(w, queue, view):
+        def load_scale_rows(w, queue, view, rows):
             by_offset = scales[w].rearrange("(j c) q n -> j c q n", j=4)
-            for q in range(16):
+            for q in rows:
                 first_row = 32 * (q // 4) + q % 4
                 queue.dma_start(
                     out=w_planes[w][first_row : first_row + 16 : 4, :, :].bitcast(view),
                     in_=by_offset[:, :, q, :].bitcast(view),
                 )
 
-        load_scale_rows(0, nc.sync, I32)
+        load_x(0)
+        load_scale_rows(0, nc.sync, I32, range(0, 6))
         load_x(1)
-        load_w_of_chunk(0, 0)
+        load_scale_rows(0, nc.sync, I32, range(6, 12))
+        load_x(2)
+        load_scale_rows(0, nc.sync, I32, range(12, 16))
+
+        bias_row = const.tile([P, 2, N], BF16)
+        nc.vector.memset(bias_row[:], 0.0)
+        for w in range(2):
+            nc.scalar.dma_start(out=bias_row[0:1, w, :], in_=biases[w].unsqueeze(0))
 
         p_index = const.tile([P, 1], I32)
         nc.gpsimd.iota(p_index[:], pattern=[[0, 1]], base=0, channel_multiplier=1)
@@ -108,7 +117,85 @@ def tile_attention_pa_k_kernel(tc, x, Wq_words, Wq_scales, bq, Wk_words, Wk_scal
         ident = const.tile([P, P], F32)
         make_identity(nc, ident[:])
 
-        load_scale_rows(1, nc.gpsimd, F32)
+        load_scale_rows(1, nc.gpsimd, F32, range(16))
+
+        q_acc = [acc_pool.tile([P, N], F32, name="q_acc_%d" % m) for m in range(TOKEN_TILES)]
+
+        codes = const.tile([P, GROUPS, TOKEN_TILES, P], U32, align_bytes=64)
+        x_plane = const.tile([P, GROUPS, TOKEN_TILES, P], U8, align_bytes=64)
+
+        def sort_words(c):
+            in_order = q_pool.tile([P, TOKEN_TILES, CHUNK, 2, P], F32, name="in_order")
+            nc.vector.tensor_copy(
+                out=in_order[:],
+                in_=x_tiles[c][:].bitcast(F32).rearrange("r m (g v u) -> r m g u v", g=CHUNK, u=2),
+            )
+            x_sorted[c] = in_order
+
+        def transpose(c):
+            in_order = x_sorted[c]
+            grouped = q_pool.tile([P, CHUNK, TOKEN_TILES, P, 4], BF16, name="grouped", align_bytes=64)
+            for g in range(CHUNK):
+                xt = t_pool.tile([P, TOKEN_TILES, 2, P], F32, name="xt", tag="xt")
+                for m in range(TOKEN_TILES):
+                    for u in range(2):
+                        nc.tensor.transpose(xt[:, m, u, :], in_order[:, m, g, u, :], ident[:])
+                nc.scalar.copy(out=grouped[:, g].bitcast(F32), in_=xt[:].rearrange("p m u r -> p m r u"))
+            x_grouped[c] = grouped
+
+        def quantise(c):
+            groups = slice(c * CHUNK, (c + 1) * CHUNK)
+            nc.vector.quantize_mx(
+                out=codes[:, groups].rearrange("p g m r -> p (g m r)").bitcast(FP8X4),
+                scales=x_plane[:, groups].rearrange("p g m r -> p (g m r)"),
+                in_=x_grouped[c][:].rearrange("p g m r t -> p (g m r t)"),
+            )
+
+        def multiply(w, piece, first_column, sums):
+            w_sb = w_tiles[(w, piece, first_column)]
+            for m in range(TOKEN_TILES):
+                for g in range(PIECE):
+                    group = piece * PIECE + g
+                    planes = w_planes[w][4 * (group // PLANES_PER_OFFSET) : P, group % PLANES_PER_OFFSET, :]
+                    done = 0
+                    for total in sums[m]:
+                        width = total.shape[1]
+                        nc.tensor.matmul_mx(
+                            out=total,
+                            lhsT=codes[:, group, m, :].bitcast(FP8X4),
+                            lhsT_scale=x_plane[:, group, m, :],
+                            rhs=w_sb[:, g, done : done + width].bitcast(FP8X4),
+                            rhs_scale=planes[:, first_column + done : first_column + done + width],
+                            start=(group == 0),
+                            stop=(group == GROUPS - 1),
+                        )
+                        done += width
+
+        sort_words(0)
+        transpose(0)
+        for c in range(1, LEAD):
+            sort_words(c)
+            transpose(c)
+            quantise(c - 1)
+        for c in range(CHUNKS):
+            load_w_of_chunk(0, c)
+            ahead = c + LEAD
+            if ahead < CHUNKS:
+                load_x(ahead)
+                sort_words(ahead)
+            if ahead - 1 < CHUNKS:
+                quantise(ahead - 1)
+            for piece in range(c * CHUNK // PIECE, (c + 1) * CHUNK // PIECE):
+                multiply(0, piece, 0, [[total[:]] for total in q_acc])
+            if ahead < CHUNKS:
+                transpose(ahead)
+
+        whole_pieces = PIECES - LAST_PIECES
+        for piece in range(whole_pieces):
+            load_w(1, piece)
+        for part in range(PARTS):
+            for piece in range(whole_pieces, PIECES):
+                load_w(1, piece, part * N_PART, N_PART)
 
         ones = const.tile([P, P], BF16)
         nc.vector.memset(ones[:], 1.0)
@@ -145,100 +232,68 @@ def tile_attention_pa_k_kernel(tc, x, Wq_words, Wq_scales, bq, Wk_words, Wk_scal
         nc.scalar.activation(out=cos_sin[:], in_=angle[:].rearrange("p f a j -> p f (a j)"), func=ACT.Sin)
         cos_both = const.tile([P, PAIRS, 2], F32)
         nc.vector.tensor_copy(out=cos_both[:], in_=cos_sin[:, 0, :].unsqueeze(2).to_broadcast([P, PAIRS, 2]))
-        minus_sin = const.tile([P, PAIRS], F32)
-        nc.vector.tensor_scalar_mul(out=minus_sin[:], in0=cos_sin[:, 1, :], scalar1=-1.0)
+        signed_sin = const.tile([P, 2, PAIRS], F32)
+        nc.vector.tensor_scalar_mul(out=signed_sin[:, 0], in0=cos_sin[:, 1, :], scalar1=-1.0)
+        nc.vector.tensor_copy(out=signed_sin[:, 1], in_=cos_sin[:, 1, :])
 
-        cos_heads = cos_both[:].rearrange("p i e -> p (i e)").unsqueeze(1).to_broadcast([P, HEADS, HEAD_DIM])
-        sin_heads = cos_sin[:, 1, :].unsqueeze(1).to_broadcast([P, HEADS, PAIRS])
-        minus_sin_heads = minus_sin[:].unsqueeze(1).to_broadcast([P, HEADS, PAIRS])
+        cos_heads = cos_both[:].rearrange("p i e -> p (i e)").unsqueeze(1).to_broadcast([P, PART_HEADS, HEAD_DIM])
+        sin_heads = signed_sin[:].unsqueeze(2).to_broadcast([P, 2, PART_HEADS, PAIRS])
 
-        acc = {}
-        for w in range(2):
-            for m in range(TOKEN_TILES):
-                acc[(w, m)] = acc_pool.tile([P, N], F32, name="acc_%d_%d" % (w, m))
-
-        codes = const.tile([P, GROUPS, TOKEN_TILES, P], U32, align_bytes=64)
-        x_plane = const.tile([P, GROUPS, TOKEN_TILES, P], U8, align_bytes=64)
-
-        def sort_words(c):
-            in_order = q_pool.tile([P, TOKEN_TILES, CHUNK, 2, P], F32, name="in_order")
-            nc.vector.tensor_copy(
-                out=in_order[:],
-                in_=x_tiles[c][:].bitcast(F32).rearrange("r m (g v u) -> r m g u v", g=CHUNK, u=2),
-            )
-            x_sorted[c] = in_order
-
-        def transpose_and_quantise(c):
-            in_order = x_sorted[c]
-            grouped = q_pool.tile([P, CHUNK, TOKEN_TILES, P, 4], BF16, name="grouped", align_bytes=64)
-            for g in range(CHUNK):
-                xt = t_pool.tile([P, TOKEN_TILES, 2, P], F32, name="xt", tag="xt")
-                for m in range(TOKEN_TILES):
-                    for u in range(2):
-                        nc.tensor.transpose(xt[:, m, u, :], in_order[:, m, g, u, :], ident[:])
-                nc.scalar.copy(out=grouped[:, g].bitcast(F32), in_=xt[:].rearrange("p m u r -> p m r u"))
-            groups = slice(c * CHUNK, (c + 1) * CHUNK)
-            nc.vector.quantize_mx(
-                out=codes[:, groups].rearrange("p g m r -> p (g m r)").bitcast(FP8X4),
-                scales=x_plane[:, groups].rearrange("p g m r -> p (g m r)"),
-                in_=grouped[:].rearrange("p g m r t -> p (g m r t)"),
-            )
-
-        def multiply(w, piece):
-            w_sb = w_tiles[(w, piece)]
-            for m in range(TOKEN_TILES):
-                for g in range(PIECE):
-                    group = piece * PIECE + g
-                    offset = 4 * (group // PLANES_PER_OFFSET)
-                    nc.tensor.matmul_mx(
-                        out=acc[(w, m)][:],
-                        lhsT=codes[:, group, m, :].bitcast(FP8X4),
-                        lhsT_scale=x_plane[:, group, m, :],
-                        rhs=w_sb[:, g, :].bitcast(FP8X4),
-                        rhs_scale=w_planes[w][offset:P, group % PLANES_PER_OFFSET, :],
-                        start=(group == 0),
-                        stop=(group == GROUPS - 1),
-                    )
-
-        def finish(w, m):
-            y = end_pool.tile([P, N], F32, name="y")
-            nc.vector.tensor_add(out=y[:], in0=acc[(w, m)][:], in1=bias_all[:, w, :])
-            straight = end_pool.tile([P, N], F32, name="straight")
+        def rotate_straight(y):
+            straight = end_pool.tile([P, N_PART], F32, name="straight")
             nc.vector.tensor_mul(
-                out=straight[:].rearrange("p (h d) -> p h d", h=HEADS),
-                in0=y[:].rearrange("p (h d) -> p h d", h=HEADS),
+                out=straight[:].rearrange("p (h d) -> p h d", h=PART_HEADS),
+                in0=y.rearrange("p (h d) -> p h d", h=PART_HEADS),
                 in1=cos_heads,
             )
-            y_pairs = y[:].rearrange("p (h i e) -> p e h i", h=HEADS, e=2)
-            crossed = end_pool.tile([P, 2, HEADS, PAIRS], F32, name="crossed")
-            nc.vector.tensor_mul(out=crossed[:, 0], in0=y_pairs[:, 1], in1=minus_sin_heads)
-            nc.vector.tensor_mul(out=crossed[:, 1], in0=y_pairs[:, 0], in1=sin_heads)
-            rotated = end_pool.tile([P, N], F32, name="rotated")
+            return straight
+
+        def rotate_crossed(y):
+            crossed = end_pool.tile([P, 2, PART_HEADS, PAIRS], F32, name="crossed")
+            nc.vector.tensor_mul(
+                out=crossed[:],
+                in0=y.rearrange("p (h i e) -> p e h i", h=PART_HEADS, e=2)[:, ::-1],
+                in1=sin_heads,
+            )
+            return crossed
+
+        def add_crossed(out, straight, crossed):
             nc.vector.tensor_add(
-                out=rotated[:].rearrange("p (n e) -> p n e", e=2),
-                in0=straight[:].rearrange("p (n e) -> p n e", e=2),
+                out=out.rearrange("p (n e) -> p n e", e=2),
+                in0=straight.rearrange("p (n e) -> p n e", e=2),
                 in1=crossed[:].rearrange("p e h i -> p (h i) e"),
             )
-            nc.sync.dma_start(out=outs[w][m * P : (m + 1) * P, :], in_=rotated[:])
 
-        sort_words(0)
-        sort_words(1)
-        transpose_and_quantise(0)
-        for c in range(CHUNKS):
-            if c + 2 < CHUNKS:
-                load_x(c + 2)
-                sort_words(c + 2)
-            if c + 1 < CHUNKS:
-                load_w_of_chunk(0, c + 1)
-                transpose_and_quantise(c + 1)
-            for piece in range(c * CHUNK // PIECE, (c + 1) * CHUNK // PIECE):
-                multiply(0, piece)
+        bias_rotated = const.tile([P, 2, PARTS, N_PART], F32)
+        for w in range(2):
+            for part in range(PARTS):
+                y = bias_all[:, w, part * N_PART : (part + 1) * N_PART]
+                straight = rotate_straight(y)
+                crossed = rotate_crossed(y)
+                add_crossed(bias_rotated[:, w, part, :], straight[:], crossed)
 
-        for piece in range(PIECES):
-            load_w(1, piece)
-        for m in range(TOKEN_TILES):
-            finish(0, m)
-        for piece in range(PIECES):
-            multiply(1, piece)
-        for m in range(TOKEN_TILES):
-            finish(1, m)
+        def finish(w, part, sums):
+            for m in range(TOKEN_TILES):
+                straight = rotate_straight(sums[m])
+                crossed = rotate_crossed(sums[m])
+                biased = end_pool.tile([P, N_PART], F32, name="biased")
+                nc.vector.tensor_add(out=biased[:], in0=straight[:], in1=bias_rotated[:, w, part, :])
+                rotated = end_pool.tile([P, N_PART], F32, name="rotated")
+                add_crossed(rotated[:], biased[:], crossed)
+                nc.sync.dma_start(
+                    out=outs[w][m * P : (m + 1) * P, part * N_PART : (part + 1) * N_PART], in_=rotated[:]
+                )
+
+        for part in range(PARTS):
+            finish(0, part, [total[:, part * N_PART : (part + 1) * N_PART] for total in q_acc])
+
+        k_acc = [
+            [t_pool.tile([P, N_PART], F32, name="k_acc", tag="xt")[:] for part in range(PARTS)] for m in range(TOKEN_TILES)
+        ]
+        for piece in range(whole_pieces):
+            multiply(1, piece, 0, k_acc)
+        for part in range(PARTS):
+            part_acc = [k_acc[m][part] for m in range(TOKEN_TILES)]
+            for piece in range(whole_pieces, PIECES):
+                multiply(1, piece, part * N_PART, [[total] for total in part_acc])
+            finish(1, part, part_acc)

@@ -89,21 +89,16 @@ def tile_attention_pa_k_kernel(tc, x, Wq_words, Wq_scales, bq, Wk_words, Wk_scal
             nc.vector.memset(planes[:].rearrange("p c n -> p (c n)").bitcast(I32), 0)
             w_planes.append(planes)
 
-        def load_scale_rows(w, queue, view, rows):
+        for w in range(2):
             by_offset = scales[w].rearrange("(j c) q n -> j c q n", j=4)
-            for q in rows:
+            for q in range(16):
                 first_row = 32 * (q // 4) + q % 4
-                queue.dma_start(
-                    out=w_planes[w][first_row : first_row + 16 : 4, :, :].bitcast(view),
-                    in_=by_offset[:, :, q, :].bitcast(view),
+                nc.sync.dma_start(
+                    out=w_planes[w][first_row : first_row + 16 : 4, :, :].bitcast(I32),
+                    in_=by_offset[:, :, q, :].bitcast(I32),
                 )
-
-        load_x(0)
-        load_scale_rows(0, nc.sync, I32, range(0, 6))
-        load_x(1)
-        load_scale_rows(0, nc.sync, I32, range(6, 12))
-        load_x(2)
-        load_scale_rows(0, nc.sync, I32, range(12, 16))
+        for c in range(LEAD):
+            load_x(c)
 
         bias_row = const.tile([P, 2, N], BF16)
         nc.vector.memset(bias_row[:], 0.0)
@@ -116,8 +111,6 @@ def tile_attention_pa_k_kernel(tc, x, Wq_words, Wq_scales, bq, Wk_words, Wk_scal
         nc.gpsimd.iota(j_index[:], pattern=[[1, FREQS]], base=0, channel_multiplier=0)
         ident = const.tile([P, P], F32)
         make_identity(nc, ident[:])
-
-        load_scale_rows(1, nc.gpsimd, F32, range(16))
 
         q_acc = [acc_pool.tile([P, N], F32, name="q_acc_%d" % m) for m in range(TOKEN_TILES)]
 

@@ -56,6 +56,7 @@ def tile_attention_pa_k_kernel(tc, x, Wq_words, Wq_scales, bq, Wk_words, Wk_scal
         w_pool = ctx.enter_context(tc.tile_pool(name="w_pool", bufs=PIECES))
         q_pool = ctx.enter_context(tc.tile_pool(name="q_pool", bufs=2))
         end_pool = ctx.enter_context(tc.tile_pool(name="end_pool", bufs=2))
+        out_pool = ctx.enter_context(tc.tile_pool(name="out_pool", bufs=2 * PARTS * TOKEN_TILES))
         acc_pool = ctx.enter_context(tc.psum_pool(name="acc_pool", bufs=1))
         t_pool = ctx.enter_context(tc.psum_pool(name="t_pool", bufs=6))
 
@@ -89,7 +90,7 @@ def tile_attention_pa_k_kernel(tc, x, Wq_words, Wq_scales, bq, Wk_words, Wk_scal
             nc.vector.memset(planes[:].rearrange("p c n -> p (c n)").bitcast(I32), 0)
             w_planes.append(planes)
 
-        for w in range(2):
+        def load_scale_rows(w):
             by_offset = scales[w].rearrange("(j c) q n -> j c q n", j=4)
             for q in range(16):
                 first_row = 32 * (q // 4) + q % 4
@@ -97,8 +98,10 @@ def tile_attention_pa_k_kernel(tc, x, Wq_words, Wq_scales, bq, Wk_words, Wk_scal
                     out=w_planes[w][first_row : first_row + 16 : 4, :, :].bitcast(I32),
                     in_=by_offset[:, :, q, :].bitcast(I32),
                 )
+
         for c in range(LEAD):
             load_x(c)
+        load_scale_rows(0)
 
         bias_row = const.tile([P, 2, N], BF16)
         nc.vector.memset(bias_row[:], 0.0)
@@ -183,6 +186,7 @@ def tile_attention_pa_k_kernel(tc, x, Wq_words, Wq_scales, bq, Wk_words, Wk_scal
             if ahead < CHUNKS:
                 transpose(ahead)
 
+        load_scale_rows(1)
         whole_pieces = PIECES - LAST_PIECES
         for piece in range(whole_pieces):
             load_w(1, piece)
@@ -271,7 +275,7 @@ def tile_attention_pa_k_kernel(tc, x, Wq_words, Wq_scales, bq, Wk_words, Wk_scal
                 crossed = rotate_crossed(sums[m])
                 biased = end_pool.tile([P, N_PART], F32, name="biased")
                 nc.vector.tensor_add(out=biased[:], in0=straight[:], in1=bias_rotated[:, w, part, :])
-                rotated = end_pool.tile([P, N_PART], F32, name="rotated")
+                rotated = out_pool.tile([P, N_PART], F32, name="rotated")
                 add_crossed(rotated[:], biased[:], crossed)
                 nc.sync.dma_start(
                     out=outs[w][m * P : (m + 1) * P, part * N_PART : (part + 1) * N_PART], in_=rotated[:]

@@ -30,9 +30,10 @@ FREQS = PAIRS // 2
 GRID = 8
 BASE = 100.0
 
-CHUNK = 4
+CHUNK = 8
+BANK_GROUPS = 2
 CHUNKS = GROUPS // CHUNK
-LEAD = 3
+SORTED_AHEAD = 2
 PIECE = 2
 PIECES = GROUPS // PIECE
 LAST_PIECES = 4
@@ -54,21 +55,24 @@ def tile_attention_pa_k_kernel(tc, x, Wq_words, Wq_scales, bq, Wk_words, Wk_scal
         const = ctx.enter_context(tc.tile_pool(name="const", bufs=1))
         x_pool = ctx.enter_context(tc.tile_pool(name="x_pool", bufs=4))
         w_pool = ctx.enter_context(tc.tile_pool(name="w_pool", bufs=PIECES))
+        sort_pool = ctx.enter_context(tc.tile_pool(name="sort_pool", bufs=SORTED_AHEAD + 1))
         q_pool = ctx.enter_context(tc.tile_pool(name="q_pool", bufs=2))
         end_pool = ctx.enter_context(tc.tile_pool(name="end_pool", bufs=2))
         out_pool = ctx.enter_context(tc.tile_pool(name="out_pool", bufs=2 * PARTS * TOKEN_TILES))
         acc_pool = ctx.enter_context(tc.psum_pool(name="acc_pool", bufs=1))
         t_pool = ctx.enter_context(tc.psum_pool(name="t_pool", bufs=6))
 
+        units = [(m, c) for c in range(CHUNKS) for m in range(TOKEN_TILES)]
         x_tiles = {}
         x_sorted = {}
         x_grouped = {}
         w_tiles = {}
 
-        def load_x(c):
-            x_sb = x_pool.tile([P, TOKEN_TILES, CHUNK * K_PASS], BF16, name="x_sb")
-            nc.sync.dma_start(out=x_sb[:], in_=x_rows[:, :, c * CHUNK * K_PASS : (c + 1) * CHUNK * K_PASS])
-            x_tiles[c] = x_sb
+        def load_x(unit):
+            m, c = unit
+            x_sb = x_pool.tile([P, CHUNK * K_PASS], BF16, name="x_sb")
+            nc.sync.dma_start(out=x_sb[:], in_=x_rows[:, m, c * CHUNK * K_PASS : (c + 1) * CHUNK * K_PASS])
+            x_tiles[unit] = x_sb
 
         def load_w(w, piece, first_column=0, columns=N):
             w_sb = w_pool.tile([P, PIECE, columns], U32, name="w_sb", align_bytes=64)
@@ -80,28 +84,28 @@ def tile_attention_pa_k_kernel(tc, x, Wq_words, Wq_scales, bq, Wk_words, Wk_scal
             )
             w_tiles[(w, piece, first_column)] = w_sb
 
-        def load_w_of_chunk(w, c):
-            for piece in range(c * CHUNK // PIECE, (c + 1) * CHUNK // PIECE):
-                load_w(w, piece)
-
         w_planes = []
         for w in range(2):
             planes = const.tile([P, PLANES_PER_OFFSET, N], U8, name="planes%d" % w, align_bytes=64)
-            nc.vector.memset(planes[:].rearrange("p c n -> p (c n)").bitcast(I32), 0)
             w_planes.append(planes)
 
-        def load_scale_rows(w):
+        def zero_planes(w):
+            nc.vector.memset(w_planes[w][:].rearrange("p c n -> p (c n)").bitcast(I32), 0)
+
+        zero_planes(0)
+
+        def load_scale_rows(w, queue, view):
             by_offset = scales[w].rearrange("(j c) q n -> j c q n", j=4)
             for q in range(16):
                 first_row = 32 * (q // 4) + q % 4
-                nc.sync.dma_start(
-                    out=w_planes[w][first_row : first_row + 16 : 4, :, :].bitcast(I32),
-                    in_=by_offset[:, :, q, :].bitcast(I32),
+                queue.dma_start(
+                    out=w_planes[w][first_row : first_row + 16 : 4, :, :].bitcast(view),
+                    in_=by_offset[:, :, q, :].bitcast(view),
                 )
 
-        for c in range(LEAD):
-            load_x(c)
-        load_scale_rows(0)
+        for unit in units:
+            load_x(unit)
+        load_scale_rows(0, nc.sync, I32)
 
         bias_row = const.tile([P, 2, N], BF16)
         nc.vector.memset(bias_row[:], 0.0)
@@ -117,34 +121,37 @@ def tile_attention_pa_k_kernel(tc, x, Wq_words, Wq_scales, bq, Wk_words, Wk_scal
 
         q_acc = [acc_pool.tile([P, N], F32, name="q_acc_%d" % m) for m in range(TOKEN_TILES)]
 
-        codes = const.tile([P, GROUPS, TOKEN_TILES, P], U32, align_bytes=64)
-        x_plane = const.tile([P, GROUPS, TOKEN_TILES, P], U8, align_bytes=64)
+        codes = const.tile([P, TOKEN_TILES, GROUPS, P], U32, align_bytes=64)
+        x_plane = const.tile([P, TOKEN_TILES, GROUPS, P], U8, align_bytes=64)
 
-        def sort_words(c):
-            in_order = q_pool.tile([P, TOKEN_TILES, CHUNK, 2, P], F32, name="in_order")
+        def sort_words(unit):
+            in_order = sort_pool.tile([P, CHUNK, 2, P], F32, name="in_order")
             nc.vector.tensor_copy(
                 out=in_order[:],
-                in_=x_tiles[c][:].bitcast(F32).rearrange("r m (g v u) -> r m g u v", g=CHUNK, u=2),
+                in_=x_tiles[unit][:].bitcast(F32).rearrange("r (g v u) -> r g u v", g=CHUNK, u=2),
             )
-            x_sorted[c] = in_order
+            x_sorted[unit] = in_order
 
-        def transpose(c):
-            in_order = x_sorted[c]
-            grouped = q_pool.tile([P, CHUNK, TOKEN_TILES, P, 4], BF16, name="grouped", align_bytes=64)
-            for g in range(CHUNK):
-                xt = t_pool.tile([P, TOKEN_TILES, 2, P], F32, name="xt", tag="xt")
-                for m in range(TOKEN_TILES):
+        def transpose(unit):
+            in_order = x_sorted[unit]
+            grouped = q_pool.tile([P, CHUNK, P, 4], BF16, name="grouped", align_bytes=64)
+            for g in range(0, CHUNK, BANK_GROUPS):
+                xt = t_pool.tile([P, BANK_GROUPS, 2, P], F32, name="xt", tag="xt")
+                for d in range(BANK_GROUPS):
                     for u in range(2):
-                        nc.tensor.transpose(xt[:, m, u, :], in_order[:, m, g, u, :], ident[:])
-                nc.scalar.copy(out=grouped[:, g].bitcast(F32), in_=xt[:].rearrange("p m u r -> p m r u"))
-            x_grouped[c] = grouped
+                        nc.tensor.transpose(xt[:, d, u, :], in_order[:, g + d, u, :], ident[:])
+                nc.scalar.copy(
+                    out=grouped[:, g : g + BANK_GROUPS].bitcast(F32), in_=xt[:].rearrange("p d u r -> p d r u")
+                )
+            x_grouped[unit] = grouped
 
-        def quantise(c):
+        def quantise(unit):
+            m, c = unit
             groups = slice(c * CHUNK, (c + 1) * CHUNK)
             nc.vector.quantize_mx(
-                out=codes[:, groups].rearrange("p g m r -> p (g m r)").bitcast(FP8X4),
-                scales=x_plane[:, groups].rearrange("p g m r -> p (g m r)"),
-                in_=x_grouped[c][:].rearrange("p g m r t -> p (g m r t)"),
+                out=codes[:, m, groups].rearrange("p g r -> p (g r)").bitcast(FP8X4),
+                scales=x_plane[:, m, groups].rearrange("p g r -> p (g r)"),
+                in_=x_grouped[unit][:].rearrange("p g r t -> p (g r t)"),
             )
 
         def multiply(w, piece, first_column, sums):
@@ -158,8 +165,8 @@ def tile_attention_pa_k_kernel(tc, x, Wq_words, Wq_scales, bq, Wk_words, Wk_scal
                         width = total.shape[1]
                         nc.tensor.matmul_mx(
                             out=total,
-                            lhsT=codes[:, group, m, :].bitcast(FP8X4),
-                            lhsT_scale=x_plane[:, group, m, :],
+                            lhsT=codes[:, m, group, :].bitcast(FP8X4),
+                            lhsT_scale=x_plane[:, m, group, :],
                             rhs=w_sb[:, g, done : done + width].bitcast(FP8X4),
                             rhs_scale=planes[:, first_column + done : first_column + done + width],
                             start=(group == 0),
@@ -167,26 +174,22 @@ def tile_attention_pa_k_kernel(tc, x, Wq_words, Wq_scales, bq, Wk_words, Wk_scal
                         )
                         done += width
 
-        sort_words(0)
-        transpose(0)
-        for c in range(1, LEAD):
-            sort_words(c)
-            transpose(c)
-            quantise(c - 1)
-        for c in range(CHUNKS):
-            load_w_of_chunk(0, c)
-            ahead = c + LEAD
-            if ahead < CHUNKS:
-                load_x(ahead)
-                sort_words(ahead)
-            if ahead - 1 < CHUNKS:
-                quantise(ahead - 1)
-            for piece in range(c * CHUNK // PIECE, (c + 1) * CHUNK // PIECE):
-                multiply(0, piece, 0, [[total[:]] for total in q_acc])
-            if ahead < CHUNKS:
-                transpose(ahead)
+        for unit in units[:SORTED_AHEAD]:
+            sort_words(unit)
+        for n, unit in enumerate(units):
+            transpose(unit)
+            if n + SORTED_AHEAD < len(units):
+                sort_words(units[n + SORTED_AHEAD])
+            quantise(unit)
 
-        load_scale_rows(1)
+        zero_planes(1)
+        load_scale_rows(1, nc.gpsimd, F32)
+
+        for piece in range(PIECES):
+            load_w(0, piece)
+        for piece in range(PIECES):
+            multiply(0, piece, 0, [[total[:]] for total in q_acc])
+
         whole_pieces = PIECES - LAST_PIECES
         for piece in range(whole_pieces):
             load_w(1, piece)

@@ -94,9 +94,9 @@ def tile_attention_pa_k_kernel(tc, x, Wq_words, Wq_scales, bq, Wk_words, Wk_scal
 
         zero_planes(0)
 
-        def load_scale_rows(w, queue, view):
+        def load_scale_rows(w, queue, view, rows):
             by_offset = scales[w].rearrange("(j c) q n -> j c q n", j=4)
-            for q in range(16):
+            for q in rows:
                 first_row = 32 * (q // 4) + q % 4
                 queue.dma_start(
                     out=w_planes[w][first_row : first_row + 16 : 4, :, :].bitcast(view),
@@ -105,7 +105,7 @@ def tile_attention_pa_k_kernel(tc, x, Wq_words, Wq_scales, bq, Wk_words, Wk_scal
 
         for unit in units:
             load_x(unit)
-        load_scale_rows(0, nc.sync, I32)
+        load_scale_rows(0, nc.sync, I32, range(0, 8))
 
         bias_row = const.tile([P, 2, N], BF16)
         nc.vector.memset(bias_row[:], 0.0)
@@ -118,6 +118,8 @@ def tile_attention_pa_k_kernel(tc, x, Wq_words, Wq_scales, bq, Wk_words, Wk_scal
         nc.gpsimd.iota(j_index[:], pattern=[[1, FREQS]], base=0, channel_multiplier=0)
         ident = const.tile([P, P], F32)
         make_identity(nc, ident[:])
+
+        load_scale_rows(0, nc.gpsimd, F32, range(8, 16))
 
         q_acc = [acc_pool.tile([P, N], F32, name="q_acc_%d" % m) for m in range(TOKEN_TILES)]
 
@@ -183,13 +185,14 @@ def tile_attention_pa_k_kernel(tc, x, Wq_words, Wq_scales, bq, Wk_words, Wk_scal
             quantise(unit)
 
         zero_planes(1)
-        load_scale_rows(1, nc.gpsimd, F32)
+        load_scale_rows(1, nc.gpsimd, F32, range(8, 16))
 
         for piece in range(PIECES):
             load_w(0, piece)
         for piece in range(PIECES):
             multiply(0, piece, 0, [[total[:]] for total in q_acc])
 
+        load_scale_rows(1, nc.sync, I32, range(0, 8))
         whole_pieces = PIECES - LAST_PIECES
         for piece in range(whole_pieces):
             load_w(1, piece)

import math
from contextlib import ExitStack

import concourse.mybir as mybir
from concourse.masks import make_identity

F32 = mybir.dt.float32
BF16 = mybir.dt.bfloat16
I32 = mybir.dt.int32
U32 = mybir.dt.uint32
U8 = mybir.dt.uint8
FP8X4 = mybir.dt.float8_e4m3fn_x4
ALU = mybir.AluOpType
ACT = mybir.ActivationFunctionType

P = 128
TOKENS = 256
TOKEN_TILES = TOKENS // P
E = 16384
K_PASS = 512
GROUPS = E // K_PASS
N = 512
N_PART = N // 2
PARTS = N // N_PART
HEADS = 8
PART_HEADS = HEADS // PARTS
HEAD_DIM = 64
PAIRS = HEAD_DIM // 2
FREQS = PAIRS // 2
GRID = 8
BASE = 100.0

CHUNK = 8
BANK_GROUPS = 2
CHUNKS = GROUPS // CHUNK
SORTED_AHEAD = 2
PIECE = 2
PIECES = GROUPS // PIECE
LAST_PIECES = 4
PLANES_PER_OFFSET = GROUPS // 4

FLOPS = 2 * TOKENS * E * 2 * N


def tile_attention_pa_k_kernel(tc, x, Wq_words, Wq_scales, bq, Wk_words, Wk_scales, bk, out_0, out_1):
    nc = tc.nc
    x_rows = x.flatten_outer_dims().rearrange("(m p) k -> p m k", p=P)
    words = [w.rearrange("g p n t -> p g (n t)") for w in (Wq_words, Wk_words)]
    scales = [Wq_scales, Wk_scales]
    biases = [bq, bk]
    outs = [o.rearrange("b s h d -> (b s) (h d)") for o in (out_0, out_1)]

    with ExitStack() as ctx:
        ctx.enter_context(tc.manual_schedule())
        const = ctx.enter_context(tc.tile_pool(name="const", bufs=1))
        x_pool = ctx.enter_context(tc.tile_pool(name="x_pool", bufs=4))
        w_pool = ctx.enter_context(tc.tile_pool(name="w_pool", bufs=PIECES))
        sort_pool = ctx.enter_context(tc.tile_pool(name="sort_pool", bufs=SORTED_AHEAD + 1))
        q_pool = ctx.enter_context(tc.tile_pool(name="q_pool", bufs=2))
        end_pool = ctx.enter_context(tc.tile_pool(name="end_pool", bufs=2))
        out_pool = ctx.enter_context(tc.tile_pool(name="out_pool", bufs=2 * PARTS * TOKEN_TILES))
        acc_pool = ctx.enter_context(tc.psum_pool(name="acc_pool", bufs=1))
        t_pool = ctx.enter_context(tc.psum_pool(name="t_pool", bufs=6))

        units = [(m, c) for c in range(CHUNKS) for m in range(TOKEN_TILES)]
        x_tiles = {}
        x_sorted = {}
        x_grouped = {}
        w_tiles = {}

        def load_x(unit):
            m, c = unit
            x_sb = x_pool.tile([P, CHUNK * K_PASS], BF16, name="x_sb")
            nc.sync.dma_start(out=x_sb[:], in_=x_rows[:, m, c * CHUNK * K_PASS : (c + 1) * CHUNK * K_PASS])
            x_tiles[unit] = x_sb

        def load_w(w, piece, first_column=0, columns=N):
            w_sb = w_pool.tile([P, PIECE, columns], U32, name="w_sb", align_bytes=64)
            nc.sync.dma_start(
                out=w_sb[:].bitcast(I32),
                in_=words[w][
                    :, piece * PIECE : (piece + 1) * PIECE, 4 * first_column : 4 * (first_column + columns)
                ].bitcast(I32),
            )
            w_tiles[(w, piece, first_column)] = w_sb

        w_planes = []
        for w in range(2):
            planes = const.tile([P, PLANES_PER_OFFSET, N], U8, name="planes%d" % w, align_bytes=64)
            w_planes.append(planes)

        def zero_planes(w):
            nc.vector.memset(w_planes[w][:].rearrange("p c n -> p (c n)").bitcast(I32), 0)

        zero_planes(0)

        def load_scale_rows(w, queue, view, rows):
            by_offset = scales[w].rearrange("(j c) q n -> j c q n", j=4)
            for q in rows:
                first_row = 32 * (q // 4) + q % 4
                queue.dma_start(
                    out=w_planes[w][first_row : first_row + 16 : 4, :, :].bitcast(view),
                    in_=by_offset[:, :, q, :].bitcast(view),
                )

        for unit in units:
            load_x(unit)
        load_scale_rows(0, nc.sync, I32, range(0, 8))

        bias_row = const.tile([P, 2, N], BF16)
        nc.vector.memset(bias_row[:], 0.0)
        for w in range(2):
            nc.scalar.dma_start(out=bias_row[0:1, w, :], in_=biases[w].unsqueeze(0))

        p_index = const.tile([P, 1], I32)
        nc.gpsimd.iota(p_index[:], pattern=[[0, 1]], base=0, channel_multiplier=1)
        j_index = const.tile([P, FREQS], I32)
        nc.gpsimd.iota(j_index[:], pattern=[[1, FREQS]], base=0, channel_multiplier=0)
        ident = const.tile([P, P], F32)
        make_identity(nc, ident[:])

        load_scale_rows(0, nc.gpsimd, F32, range(8, 16))

        q_acc = [acc_pool.tile([P, N], F32, name="q_acc_%d" % m) for m in range(TOKEN_TILES)]

        codes = const.tile([P, TOKEN_TILES, GROUPS, P], U32, align_bytes=64)
        x_plane = const.tile([P, TOKEN_TILES, GROUPS, P], U8, align_bytes=64)

        def sort_words(unit):
            in_order = sort_pool.tile([P, CHUNK, 2, P], F32, name="in_order")
            nc.vector.tensor_copy(
                out=in_order[:],
                in_=x_tiles[unit][:].bitcast(F32).rearrange("r (g v u) -> r g u v", g=CHUNK, u=2),
            )
            x_sorted[unit] = in_order

        def transpose(unit):
            in_order = x_sorted[unit]
            grouped = q_pool.tile([P, CHUNK, P, 4], BF16, name="grouped", align_bytes=64)
            for g in range(0, CHUNK, BANK_GROUPS):
                xt = t_pool.tile([P, BANK_GROUPS, 2, P], F32, name="xt", tag="xt")
                for d in range(BANK_GROUPS):
                    for u in range(2):
                        nc.tensor.transpose(xt[:, d, u, :], in_order[:, g + d, u, :], ident[:])
                nc.scalar.copy(
                    out=grouped[:, g : g + BANK_GROUPS].bitcast(F32), in_=xt[:].rearrange("p d u r -> p d r u")
                )
            x_grouped[unit] = grouped

        def quantise(unit):
            m, c = unit
            groups = slice(c * CHUNK, (c + 1) * CHUNK)
            nc.vector.quantize_mx(
                out=codes[:, m, groups].rearrange("p g r -> p (g r)").bitcast(FP8X4),
                scales=x_plane[:, m, groups].rearrange("p g r -> p (g r)"),
                in_=x_grouped[unit][:].rearrange("p g r t -> p (g r t)"),
            )

        def multiply(w, piece, first_column, sums):
            w_sb = w_tiles[(w, piece, first_column)]
            for m in range(TOKEN_TILES):
                for g in range(PIECE):
                    group = piece * PIECE + g
                    planes = w_planes[w][4 * (group // PLANES_PER_OFFSET) : P, group % PLANES_PER_OFFSET, :]
                    done = 0
                    for total in sums[m]:
                        width = total.shape[1]
                        nc.tensor.matmul_mx(
                            out=total,
                            lhsT=codes[:, m, group, :].bitcast(FP8X4),
                            lhsT_scale=x_plane[:, m, group, :],
                            rhs=w_sb[:, g, done : done + width].bitcast(FP8X4),
                            rhs_scale=planes[:, first_column + done : first_column + done + width],
                            start=(group == 0),
                            stop=(group == GROUPS - 1),
                        )
                        done += width

        for unit in units[:SORTED_AHEAD]:
            sort_words(unit)
        for n, unit in enumerate(units):
            transpose(unit)
            if n + SORTED_AHEAD < len(units):
                sort_words(units[n + SORTED_AHEAD])
            quantise(unit)

        zero_planes(1)
        load_scale_rows(1, nc.gpsimd, F32, range(8, 16))

        for piece in range(PIECES):
            load_w(0, piece)
        for piece in range(PIECES):
            multiply(0, piece, 0, [[total[:]] for total in q_acc])

        load_scale_rows(1, nc.sync, I32, range(0, 8))
        whole_pieces = PIECES - LAST_PIECES
        for piece in range(whole_pieces):
            load_w(1, piece)
        for part in range(PARTS):
            for piece in range(whole_pieces, PIECES):
                load_w(1, piece, part * N_PART, N_PART)

        ones = const.tile([P, P], BF16)
        nc.vector.memset(ones[:], 1.0)
        bias_all = const.tile([P, 2, N], F32)
        for w in range(2):
            bias_ps = t_pool.tile([P, N], F32, name="bias_ps", tag="xt")
            nc.tensor.matmul(out=bias_ps[:], lhsT=ones[:], rhs=bias_row[:, w, :], start=True, stop=True)
            nc.vector.tensor_copy(out=bias_all[:, w, :], in_=bias_ps[:])

        pos_int = const.tile([P, 2], I32)
        nc.vector.tensor_scalar(
            out=pos_int[:, 0:1], in0=p_index[:], scalar1=3, scalar2=GRID - 1,
            op0=ALU.logical_shift_right, op1=ALU.bitwise_and,
        )
        nc.vector.tensor_single_scalar(out=pos_int[:, 1:2], in_=p_index[:], scalar=GRID - 1, op=ALU.bitwise_and)
        pos = const.tile([P, 2], F32)
        nc.vector.tensor_copy(out=pos[:], in_=pos_int[:])
        j_float = const.tile([P, FREQS], F32)
        nc.vector.tensor_copy(out=j_float[:], in_=j_index[:])
        freq = const.tile([P, FREQS], F32)
        nc.scalar.activation(out=freq[:], in_=j_float[:], func=ACT.Exp, scale=-math.log(BASE) / FREQS)
        angle = const.tile([P, 2, 2, FREQS], F32)
        for half in range(2):
            nc.vector.tensor_scalar(
                out=angle[:, 1, half, :], in0=freq[:], scalar1=pos[:, half : half + 1], scalar2=None, op0=ALU.mult
            )
        nc.vector.tensor_scalar_add(out=angle[:, 0], in0=angle[:, 1], scalar1=math.pi / 2)
        turn = const.tile([P, 2, 2, FREQS], F32)
        nc.vector.tensor_scalar(
            out=turn[:], in0=angle[:], scalar1=math.pi, scalar2=2 * math.pi, op0=ALU.is_gt, op1=ALU.mult
        )
        nc.vector.tensor_sub(out=angle[:], in0=angle[:], in1=turn[:])
        cos_sin = const.tile([P, 2, PAIRS], F32)
        nc.scalar.activation(out=cos_sin[:], in_=angle[:].rearrange("p f a j -> p f (a j)"), func=ACT.Sin)
        cos_both = const.tile([P, PAIRS, 2], F32)
        nc.vector.tensor_copy(out=cos_both[:], in_=cos_sin[:, 0, :].unsqueeze(2).to_broadcast([P, PAIRS, 2]))
        signed_sin = const.tile([P, 2, PAIRS], F32)
        nc.vector.tensor_scalar_mul(out=signed_sin[:, 0], in0=cos_sin[:, 1, :], scalar1=-1.0)
        nc.vector.tensor_copy(out=signed_sin[:, 1], in_=cos_sin[:, 1, :])

        cos_heads = cos_both[:].rearrange("p i e -> p (i e)").unsqueeze(1).to_broadcast([P, PART_HEADS, HEAD_DIM])
        sin_heads = signed_sin[:].unsqueeze(2).to_broadcast([P, 2, PART_HEADS, PAIRS])

        def rotate_straight(y):
            straight = end_pool.tile([P, N_PART], F32, name="straight")
            nc.vector.tensor_mul(
                out=straight[:].rearrange("p (h d) -> p h d", h=PART_HEADS),
                in0=y.rearrange("p (h d) -> p h d", h=PART_HEADS),
                in1=cos_heads,
            )
            return straight

        def rotate_crossed(y):
            crossed = end_pool.tile([P, 2, PART_HEADS, PAIRS], F32, name="crossed")
            nc.vector.tensor_mul(
                out=crossed[:],
                in0=y.rearrange("p (h i e) -> p e h i", h=PART_HEADS, e=2)[:, ::-1],
                in1=sin_heads,
            )
            return crossed

        def add_crossed(out, straight, crossed):
            nc.vector.tensor_add(
                out=out.rearrange("p (n e) -> p n e", e=2),
                in0=straight.rearrange("p (n e) -> p n e", e=2),
                in1=crossed[:].rearrange("p e h i -> p (h i) e"),
            )

        bias_rotated = const.tile([P, 2, PARTS, N_PART], F32)
        for w in range(2):
            for part in range(PARTS):
                y = bias_all[:, w, part * N_PART : (part + 1) * N_PART]
                straight = rotate_straight(y)
                crossed = rotate_crossed(y)
                add_crossed(bias_rotated[:, w, part, :], straight[:], crossed)

        def finish(w, part, sums):
            for m in range(TOKEN_TILES):
                straight = rotate_straight(sums[m])
                crossed = rotate_crossed(sums[m])
                biased = end_pool.tile([P, N_PART], F32, name="biased")
                nc.vector.tensor_add(out=biased[:], in0=straight[:], in1=bias_rotated[:, w, part, :])
                rotated = out_pool.tile([P, N_PART], F32, name="rotated")
                add_crossed(rotated[:], biased[:], crossed)
                nc.sync.dma_start(
                    out=outs[w][m * P : (m + 1) * P, part * N_PART : (part + 1) * N_PART], in_=rotated[:]
                )

        for part in range(PARTS):
            finish(0, part, [total[:, part * N_PART : (part + 1) * N_PART] for total in q_acc])

        k_acc = [
            [t_pool.tile([P, N_PART], F32, name="k_acc", tag="xt")[:] for part in range(PARTS)] for m in range(TOKEN_TILES)
        ]
        for piece in range(whole_pieces):
            multiply(1, piece, 0, k_acc)
        for part in range(PARTS):
            part_acc = [k_acc[m][part] for m in range(TOKEN_TILES)]
            for piece in range(whole_pieces, PIECES):
                multiply(1, piece, part * N_PART, [[total] for total in part_acc])
            finish(1, part, part_acc)
